import numpy as np
import ml_dtypes


def mxq(x, axis, fmt="e4m3"):
    dtype, down = {"e4m3": (ml_dtypes.float8_e4m3fn, 7), "e5m2": (ml_dtypes.float8_e5m2, 14)}[fmt]
    v = np.moveaxis(np.asarray(x, np.float32).astype(ml_dtypes.bfloat16).astype(np.float64), axis, -1)
    blocks = v.reshape(v.shape[:-1] + (-1, 32))
    amax = np.abs(blocks).max(-1, keepdims=True)
    byte = np.maximum(np.where(amax > 0, np.frexp(amax)[1] - 1 + 127, 0) - down, 1)
    scale = np.exp2(byte - 127.0)
    codes = (blocks / scale).astype(np.float32).astype(dtype).astype(np.float64)
    return np.moveaxis((codes * scale).reshape(v.shape), -1, axis)


WIDE = False


def mx_kscale(k):
    if not WIDE:
        return np.ones(k)
    levels = np.array([10, -10, 5, -5, 0])
    a = np.random.permutation(np.resize(levels, k // 512 * 4)).reshape(k // 512, 4)
    idx = np.arange(k)
    return np.exp2(a[idx // 512, idx % 128 // 32])


BF16 = ml_dtypes.bfloat16


def bf(x):
    return np.asarray(x, np.float32).astype(BF16)


def f64(x):
    return np.asarray(x).astype(np.float64)


E2M1 = np.array([0.0, 0.5, 1.0, 1.5, 2.0, 3.0, 4.0, 6.0, -0.0, -0.5, -1.0, -1.5, -2.0, -3.0, -4.0, -6.0])


def pack_weight(w, fmt):
    k, n = w.shape
    w = f64(bf(w)).reshape(k // 32, 32, n)
    amax = np.abs(w).max(1)
    if fmt == "e4m3":
        byte = np.frexp(amax)[1] - 1 + 127 - 7
    else:
        mant, ex = np.frexp(amax / 6.0)
        byte = np.where(mant > 0.5, ex, ex - 1) + 127
    byte = np.clip(np.where(amax > 0, byte, 1), 1, 254)
    scaled = (w * np.exp2(127.0 - byte)[:, None, :]).reshape(k, n).astype(np.float32)
    by_word = np.ascontiguousarray(scaled.reshape(k // 512, 128, 4, n).transpose(0, 1, 3, 2))
    if fmt == "e4m3":
        words = by_word.astype(ml_dtypes.float8_e4m3fn).view(np.uint8)
    else:
        c = by_word.astype(ml_dtypes.float4_e2m1fn).view(np.uint8) & 0xF
        words = c[..., 0::2] | (c[..., 1::2] << 4)
    return np.ascontiguousarray(words), np.ascontiguousarray(byte.astype(np.uint8).reshape(k // 512, 16, n))


def unpack_weight(words, scales, fmt):
    g, p, n, _ = words.shape
    if fmt == "e4m3":
        vals = np.ascontiguousarray(words).view(ml_dtypes.float8_e4m3fn).astype(np.float64)
    else:
        nib = np.empty((g, p, n, 4), np.uint8)
        nib[..., 0::2] = words & 0xF
        nib[..., 1::2] = words >> 4
        vals = E2M1[nib]
    vals = vals * np.repeat(np.exp2(scales.astype(np.float64) - 127.0), 8, axis=1)[..., None]
    return vals.transpose(0, 1, 3, 2).reshape(g * 512, n)


B, D, K = 128, 3072, 2


def setup_inputs():
    s = mx_kscale(D)
    x = np.random.standard_normal((B, D, K)) * s[None, :, None]
    mu = np.random.standard_normal((D, K)) * 0.3 * s[:, None]
    w = (np.eye(D)[None] + np.random.standard_normal((K, D, D)) * 0.7 / np.sqrt(D)) / s[None, None, :]
    cat = np.ascontiguousarray(w.swapaxes(1, 2)).reshape(-1, D)
    words, scales = pack_weight(cat, "e4m3")
    return {"x": bf(x), "mu_track": bf(mu), "Std_inv_track_words": words, "Std_inv_track_scales": scales}


def reference(x, mu_track, Std_inv_track_words, Std_inv_track_scales):
    x_cnt = f64(x) - f64(mu_track)[None]
    xq = mxq(x_cnt, 1, "e4m3")
    wq = unpack_weight(Std_inv_track_words, Std_inv_track_scales, "e4m3").reshape(K, D, D).swapaxes(1, 2)
    z = wq @ xq.transpose(2, 1, 0)
    return z.transpose(2, 1, 0)

@@ -1,0 +1,134 @@
+from contextlib import ExitStack
+
+import concourse.mybir as mybir
+from concourse.masks import make_identity
+
+F32 = mybir.dt.float32
+BF16 = mybir.dt.bfloat16
+I32 = mybir.dt.int32
+U32 = mybir.dt.uint32
+U8 = mybir.dt.uint8
+FP8X4 = mybir.dt.float8_e4m3fn_x4
+
+P = 128
+PACK = 4
+K_PASS = P * PACK
+FEATURES = 3072
+CLUSTERS = 2
+PASSES = FEATURES // K_PASS
+PLANES_PER_TILE = 4
+N_TILE = 256
+COLUMN_RANGES = ((0, 2048), (2048, 1024))
+
+FLOPS = 2 * P * FEATURES * FEATURES * CLUSTERS
+
+
+def tile_clusternorm1dv3_w_e_kernel(tc, x, mu_track, w_words, w_scale_rows, out):
+    nc = tc.nc
+    with ExitStack() as ctx:
+        keep = ctx.enter_context(tc.tile_pool(name="keep", bufs=1))
+        psum = ctx.enter_context(tc.psum_pool(name="psum", bufs=1))
+
+        x_sb = keep.tile([P, FEATURES * CLUSTERS], BF16)
+        nc.sync.dma_start(out=x_sb[:], in_=x.rearrange("b e c -> b (e c)"))
+
+        mean = keep.tile([P, PASSES, PACK * CLUSTERS], BF16)
+        nc.scalar.dma_start(
+            out=mean[:], in_=mu_track.rearrange("(g p t) c -> p g (t c)", p=P, t=PACK)
+        )
+
+        n_plane_tiles = CLUSTERS * PASSES // PLANES_PER_TILE
+        w_planes = keep.tile([P, n_plane_tiles, FEATURES], U8, align_bytes=64)
+        nc.vector.memset(w_planes[:].bitcast(I32), 0)
+        for a in range(n_plane_tiles):
+            for quadrant in range(4):
+                nc.sync.dma_start(
+                    out=w_planes[32 * quadrant : 32 * quadrant + 16, a, :].bitcast(I32),
+                    in_=w_scale_rows[
+                        PLANES_PER_TILE * a : PLANES_PER_TILE * (a + 1),
+                        4 * quadrant : 4 * quadrant + 4,
+                        :,
+                    ].bitcast(I32),
+                )
+
+        w_codes = {}
+        for first, width in COLUMN_RANGES:
+            for pass_no in range(CLUSTERS * PASSES):
+                codes = keep.tile([P, width], I32, name="w_codes_%d_%d" % (first, pass_no), align_bytes=64)
+                nc.sync.dma_start(
+                    out=codes[:],
+                    in_=w_words[pass_no]
+                    .rearrange("p n t -> p (n t)")[:, PACK * first : PACK * (first + width)]
+                    .bitcast(I32),
+                )
+                w_codes[(first, pass_no)] = codes
+
+        identity = keep.tile([P, P], F32)
+        make_identity(nc, identity[:])
+
+        x_pairs = x_sb[:].bitcast(F32)
+        centred = keep.tile([P, PASSES, CLUSTERS, P, PACK], BF16, align_bytes=64)
+        x_codes = keep.tile([P, PASSES, CLUSTERS, P], U32, align_bytes=64)
+        x_planes = keep.tile([P, PASSES, CLUSTERS, P], U8, align_bytes=64)
+
+        def quantise(g):
+            nc.vector.quantize_mx(
+                out=x_codes[:, g].rearrange("p c b -> p (c b)").bitcast(FP8X4),
+                scales=x_planes[:, g].rearrange("p c b -> p (c b)"),
+                in_=centred[:, g].rearrange("p c b t -> p (c b t)"),
+            )
+
+        for g in range(PASSES):
+            flipped = psum.tile([P, PACK, P], F32, tag="bank%d" % g)
+            for t in range(PACK):
+                nc.tensor.transpose(
+                    flipped[:, t, :], x_pairs[:, K_PASS * g + t : K_PASS * (g + 1) : PACK], identity[:]
+                )
+            nc.vector.tensor_tensor(
+                out=centred[:, g],
+                in0=flipped[:].bitcast(BF16).rearrange("p t (b c) -> p c b t", c=CLUSTERS),
+                in1=mean[:, g, :]
+                .rearrange("p (t c) -> p c t", c=CLUSTERS)
+                .unsqueeze(2)
+                .to_broadcast([P, CLUSTERS, P, PACK]),
+                op=mybir.AluOpType.subtract,
+            )
+            if g > 0:
+                quantise(g - 1)
+        quantise(PASSES - 1)
+
+        out_sb = keep.tile([P, FEATURES, CLUSTERS], F32)
+        for first, width in COLUMN_RANGES:
+            n_banks = width // N_TILE
+            sums = [
+                psum.tile([P, CLUSTERS, N_TILE], F32, tag="bank%d" % j, name="sums%d" % j)
+                for j in range(n_banks)
+            ]
+            for c in range(CLUSTERS):
+                for g in range(PASSES):
+                    pass_no = PASSES * c + g
+                    plane_tile = pass_no // PLANES_PER_TILE
+                    plane_start = 4 * (pass_no % PLANES_PER_TILE)
+                    for j in range(n_banks):
+                        nc.tensor.matmul_mx(
+                            out=sums[j][:, c, :],
+                            lhsT=x_codes[:, g, c, :].bitcast(FP8X4),
+                            lhsT_scale=x_planes[:, g, c, :],
+                            rhs=w_codes[(first, pass_no)][:, N_TILE * j : N_TILE * (j + 1)].bitcast(FP8X4),
+                            rhs_scale=w_planes[
+                                plane_start:P, plane_tile, first + N_TILE * j : first + N_TILE * (j + 1)
+                            ],
+                            start=(g == 0),
+                            stop=(g == PASSES - 1),
+                        )
+            for j in range(n_banks):
+                columns = out_sb[:, first + N_TILE * j : first + N_TILE * (j + 1), :]
+                interleaved = sums[j][:].rearrange("p c d -> p d c")
+                if j % 2 == 0:
+                    nc.vector.tensor_copy(out=columns, in_=interleaved)
+                else:
+                    nc.scalar.copy(out=columns, in_=interleaved)
+            nc.sync.dma_start(
+                out=out[:, first : first + width, :].rearrange("b d c -> b (d c)"),
+                in_=out_sb[:, first : first + width, :].rearrange("b d c -> b (d c)"),
+            )

@@ -18,7 +18,10 @@ CLUSTERS = 2
 PASSES = FEATURES // K_PASS
 PLANES_PER_TILE = 4
 N_TILE = 256
-COLUMN_RANGES = ((0, 2048), (2048, 1024))
+BANK = 512
+FIRST = 2048
+LAST = FEATURES - FIRST
+SPLIT_FROM = 1
 
 FLOPS = 2 * P * FEATURES * FEATURES * CLUSTERS
 
@@ -51,17 +54,22 @@ def tile_clusternorm1dv3_w_e_kernel(tc, x, mu_track, w_words, w_scale_rows, out)
                     ].bitcast(I32),
                 )
 
-        w_codes = {}
-        for first, width in COLUMN_RANGES:
-            for pass_no in range(CLUSTERS * PASSES):
-                codes = keep.tile([P, width], I32, name="w_codes_%d_%d" % (first, pass_no), align_bytes=64)
-                nc.sync.dma_start(
-                    out=codes[:],
-                    in_=w_words[pass_no]
-                    .rearrange("p n t -> p (n t)")[:, PACK * first : PACK * (first + width)]
-                    .bitcast(I32),
-                )
-                w_codes[(first, pass_no)] = codes
+        w_codes = keep.tile([P, CLUSTERS * PASSES, FEATURES], I32, align_bytes=64)
+
+        def load_words(pass_no, first, width):
+            nc.sync.dma_start(
+                out=w_codes[:, pass_no, first : first + width],
+                in_=w_words[pass_no]
+                .rearrange("p n t -> p (n t)")[:, PACK * first : PACK * (first + width)]
+                .bitcast(I32),
+            )
+
+        for pass_no in range(PASSES + SPLIT_FROM):
+            load_words(pass_no, 0, FEATURES)
+        for pass_no in range(PASSES + SPLIT_FROM, CLUSTERS * PASSES):
+            load_words(pass_no, 0, FIRST)
+        for pass_no in range(PASSES + SPLIT_FROM, CLUSTERS * PASSES):
+            load_words(pass_no, FIRST, LAST)
 
         identity = keep.tile([P, P], F32)
         make_identity(nc, identity[:])
@@ -98,37 +106,62 @@ def tile_clusternorm1dv3_w_e_kernel(tc, x, mu_track, w_words, w_scale_rows, out)
         quantise(PASSES - 1)
 
         out_sb = keep.tile([P, FEATURES, CLUSTERS], F32)
-        for first, width in COLUMN_RANGES:
-            n_banks = width // N_TILE
-            sums = [
-                psum.tile([P, CLUSTERS, N_TILE], F32, tag="bank%d" % j, name="sums%d" % j)
-                for j in range(n_banks)
-            ]
-            for c in range(CLUSTERS):
-                for g in range(PASSES):
-                    pass_no = PASSES * c + g
-                    plane_tile = pass_no // PLANES_PER_TILE
-                    plane_start = 4 * (pass_no % PLANES_PER_TILE)
-                    for j in range(n_banks):
-                        nc.tensor.matmul_mx(
-                            out=sums[j][:, c, :],
-                            lhsT=x_codes[:, g, c, :].bitcast(FP8X4),
-                            lhsT_scale=x_planes[:, g, c, :],
-                            rhs=w_codes[(first, pass_no)][:, N_TILE * j : N_TILE * (j + 1)].bitcast(FP8X4),
-                            rhs_scale=w_planes[
-                                plane_start:P, plane_tile, first + N_TILE * j : first + N_TILE * (j + 1)
-                            ],
-                            start=(g == 0),
-                            stop=(g == PASSES - 1),
-                        )
-            for j in range(n_banks):
-                columns = out_sb[:, first + N_TILE * j : first + N_TILE * (j + 1), :]
-                interleaved = sums[j][:].rearrange("p c d -> p d c")
-                if j % 2 == 0:
-                    nc.vector.tensor_copy(out=columns, in_=interleaved)
-                else:
-                    nc.scalar.copy(out=columns, in_=interleaved)
+        n_first = FIRST // BANK
+        n_last = LAST // N_TILE
+        last_sums = [
+            psum.tile([P, CLUSTERS, N_TILE], F32, tag="bank%d" % (n_first + j), name="last_sums%d" % j)
+            for j in range(n_last)
+        ]
+
+        def add_pass(c, g, sums, column, width):
+            pass_no = PASSES * c + g
+            nc.tensor.matmul_mx(
+                out=sums,
+                lhsT=x_codes[:, g, c, :].bitcast(FP8X4),
+                lhsT_scale=x_planes[:, g, c, :],
+                rhs=w_codes[:, pass_no, column : column + width].bitcast(FP8X4),
+                rhs_scale=w_planes[
+                    4 * (pass_no % PLANES_PER_TILE) : P,
+                    pass_no // PLANES_PER_TILE,
+                    column : column + width,
+                ],
+                start=(g == 0),
+                stop=(g == PASSES - 1),
+            )
+
+        def add_last(c, g):
+            for j in range(n_last):
+                add_pass(c, g, last_sums[j][:, c, :], FIRST + N_TILE * j, N_TILE)
+
+        def copy_out(j, target, source):
+            if j % 2 == 0:
+                nc.vector.tensor_copy(out=target, in_=source)
+            else:
+                nc.scalar.copy(out=target, in_=source)
+
+        def store(first, width):
             nc.sync.dma_start(
                 out=out[:, first : first + width, :].rearrange("b d c -> b (d c)"),
                 in_=out_sb[:, first : first + width, :].rearrange("b d c -> b (d c)"),
             )
+
+        for c in range(CLUSTERS):
+            first_sums = [
+                psum.tile([P, BANK], F32, tag="bank%d" % j, name="first_sums%d" % j)
+                for j in range(n_first)
+            ]
+            for g in range(PASSES):
+                for j in range(n_first):
+                    add_pass(c, g, first_sums[j][:], BANK * j, BANK)
+                if c == 0 or g < SPLIT_FROM:
+                    add_last(c, g)
+            for j in range(n_first):
+                copy_out(j, out_sb[:, BANK * j : BANK * (j + 1), c], first_sums[j][:])
+        for j in range(0, n_first, 2):
+            store(BANK * j, 2 * BANK)
+        for g in range(SPLIT_FROM, PASSES):
+            add_last(1, g)
+        for j in range(n_last):
+            first = FIRST + N_TILE * j
+            copy_out(j, out_sb[:, first : first + N_TILE, :], last_sums[j][:].rearrange("p c d -> p d c"))
+        store(FIRST, LAST)

from contextlib import ExitStack

import concourse.mybir as mybir
from concourse.masks import make_identity

F32 = mybir.dt.float32
BF16 = mybir.dt.bfloat16
I32 = mybir.dt.int32
U32 = mybir.dt.uint32
U8 = mybir.dt.uint8
FP8X4 = mybir.dt.float8_e4m3fn_x4

P = 128
PACK = 4
K_PASS = P * PACK
FEATURES = 3072
CLUSTERS = 2
PASSES = FEATURES // K_PASS
PLANES_PER_TILE = 4
N_TILE = 256
BANK = 512
FIRST = 2048
LAST = FEATURES - FIRST
SPLIT_FROM = 1

FLOPS = 2 * P * FEATURES * FEATURES * CLUSTERS


def tile_clusternorm1dv3_w_e_kernel(tc, x, mu_track, w_words, w_scale_rows, out):
    nc = tc.nc
    with ExitStack() as ctx:
        keep = ctx.enter_context(tc.tile_pool(name="keep", bufs=1))
        psum = ctx.enter_context(tc.psum_pool(name="psum", bufs=1))

        x_sb = keep.tile([P, FEATURES * CLUSTERS], BF16)
        nc.sync.dma_start(out=x_sb[:], in_=x.rearrange("b e c -> b (e c)"))

        mean = keep.tile([P, PASSES, PACK * CLUSTERS], BF16)
        nc.scalar.dma_start(
            out=mean[:], in_=mu_track.rearrange("(g p t) c -> p g (t c)", p=P, t=PACK)
        )

        n_plane_tiles = CLUSTERS * PASSES // PLANES_PER_TILE
        w_planes = keep.tile([P, n_plane_tiles, FEATURES], U8, align_bytes=64)
        nc.vector.memset(w_planes[:].bitcast(I32), 0)
        for a in range(n_plane_tiles):
            for quadrant in range(4):
                nc.sync.dma_start(
                    out=w_planes[32 * quadrant : 32 * quadrant + 16, a, :].bitcast(I32),
                    in_=w_scale_rows[
                        PLANES_PER_TILE * a : PLANES_PER_TILE * (a + 1),
                        4 * quadrant : 4 * quadrant + 4,
                        :,
                    ].bitcast(I32),
                )

        w_codes = keep.tile([P, CLUSTERS * PASSES, FEATURES], I32, align_bytes=64)

        def load_words(pass_no, first, width):
            nc.sync.dma_start(
                out=w_codes[:, pass_no, first : first + width],
                in_=w_words[pass_no]
                .rearrange("p n t -> p (n t)")[:, PACK * first : PACK * (first + width)]
                .bitcast(I32),
            )

        for pass_no in range(PASSES + SPLIT_FROM):
            load_words(pass_no, 0, FEATURES)
        for pass_no in range(PASSES + SPLIT_FROM, CLUSTERS * PASSES):
            load_words(pass_no, 0, FIRST)
        for pass_no in range(PASSES + SPLIT_FROM, CLUSTERS * PASSES):
            load_words(pass_no, FIRST, LAST)

        identity = keep.tile([P, P], F32)
        make_identity(nc, identity[:])

        x_pairs = x_sb[:].bitcast(F32)
        centred = keep.tile([P, PASSES, CLUSTERS, P, PACK], BF16, align_bytes=64)
        x_codes = keep.tile([P, PASSES, CLUSTERS, P], U32, align_bytes=64)
        x_planes = keep.tile([P, PASSES, CLUSTERS, P], U8, align_bytes=64)

        def quantise(g):
            nc.vector.quantize_mx(
                out=x_codes[:, g].rearrange("p c b -> p (c b)").bitcast(FP8X4),
                scales=x_planes[:, g].rearrange("p c b -> p (c b)"),
                in_=centred[:, g].rearrange("p c b t -> p (c b t)"),
            )

        for g in range(PASSES):
            flipped = psum.tile([P, PACK, P], F32, tag="bank%d" % g)
            for t in range(PACK):
                nc.tensor.transpose(
                    flipped[:, t, :], x_pairs[:, K_PASS * g + t : K_PASS * (g + 1) : PACK], identity[:]
                )
            nc.vector.tensor_tensor(
                out=centred[:, g],
                in0=flipped[:].bitcast(BF16).rearrange("p t (b c) -> p c b t", c=CLUSTERS),
                in1=mean[:, g, :]
                .rearrange("p (t c) -> p c t", c=CLUSTERS)
                .unsqueeze(2)
                .to_broadcast([P, CLUSTERS, P, PACK]),
                op=mybir.AluOpType.subtract,
            )
            if g > 0:
                quantise(g - 1)
        quantise(PASSES - 1)

        out_sb = keep.tile([P, FEATURES, CLUSTERS], F32)
        n_first = FIRST // BANK
        n_last = LAST // N_TILE
        last_sums = [
            psum.tile([P, CLUSTERS, N_TILE], F32, tag="bank%d" % (n_first + j), name="last_sums%d" % j)
            for j in range(n_last)
        ]

        def add_pass(c, g, sums, column, width):
            pass_no = PASSES * c + g
            nc.tensor.matmul_mx(
                out=sums,
                lhsT=x_codes[:, g, c, :].bitcast(FP8X4),
                lhsT_scale=x_planes[:, g, c, :],
                rhs=w_codes[:, pass_no, column : column + width].bitcast(FP8X4),
                rhs_scale=w_planes[
                    4 * (pass_no % PLANES_PER_TILE) : P,
                    pass_no // PLANES_PER_TILE,
                    column : column + width,
                ],
                start=(g == 0),
                stop=(g == PASSES - 1),
            )

        def add_last(c, g):
            for j in range(n_last):
                add_pass(c, g, last_sums[j][:, c, :], FIRST + N_TILE * j, N_TILE)

        def copy_out(j, target, source):
            if j % 2 == 0:
                nc.vector.tensor_copy(out=target, in_=source)
            else:
                nc.scalar.copy(out=target, in_=source)

        def store(first, width):
            nc.sync.dma_start(
                out=out[:, first : first + width, :].rearrange("b d c -> b (d c)"),
                in_=out_sb[:, first : first + width, :].rearrange("b d c -> b (d c)"),
            )

        for c in range(CLUSTERS):
            first_sums = [
                psum.tile([P, BANK], F32, tag="bank%d" % j, name="first_sums%d" % j)
                for j in range(n_first)
            ]
            for g in range(PASSES):
                for j in range(n_first):
                    add_pass(c, g, first_sums[j][:], BANK * j, BANK)
                if c == 0 or g < SPLIT_FROM:
                    add_last(c, g)
            for j in range(n_first):
                copy_out(j, out_sb[:, BANK * j : BANK * (j + 1), c], first_sums[j][:])
        for j in range(0, n_first, 2):
            store(BANK * j, 2 * BANK)
        for g in range(SPLIT_FROM, PASSES):
            add_last(1, g)
        for j in range(n_last):
            first = FIRST + N_TILE * j
            copy_out(j, out_sb[:, first : first + N_TILE, :], last_sums[j][:].rearrange("p c d -> p d c"))
        store(FIRST, LAST)
